import numpy as np
import ml_dtypes


def mxq(x, axis, fmt="e4m3"):
    dtype, down = {"e4m3": (ml_dtypes.float8_e4m3fn, 7), "e5m2": (ml_dtypes.float8_e5m2, 14)}[fmt]
    v = np.moveaxis(np.asarray(x, np.float32).astype(ml_dtypes.bfloat16).astype(np.float64), axis, -1)
    blocks = v.reshape(v.shape[:-1] + (-1, 32))
    amax = np.abs(blocks).max(-1, keepdims=True)
    byte = np.maximum(np.where(amax > 0, np.frexp(amax)[1] - 1 + 127, 0) - down, 1)
    scale = np.exp2(byte - 127.0)
    codes = (blocks / scale).astype(np.float32).astype(dtype).astype(np.float64)
    return np.moveaxis((codes * scale).reshape(v.shape), -1, axis)


WIDE = False


def mx_kscale(k):
    if not WIDE:
        return np.ones(k)
    levels = np.array([10, -10, 5, -5, 0])
    a = np.random.permutation(np.resize(levels, k // 512 * 4)).reshape(k // 512, 4)
    idx = np.arange(k)
    return np.exp2(a[idx // 512, idx % 128 // 32])


BF16 = ml_dtypes.bfloat16


def bf(x):
    return np.asarray(x, np.float32).astype(BF16)


def f64(x):
    return np.asarray(x).astype(np.float64)


B, T, D, H = 8, 1024, 512, 128
N = B * T
EMA0 = 1.0


def silu(v):
    return v / (1.0 + np.exp(-v))


def surprise_gate(err):
    err_mag = np.sqrt(np.sum(err * err)) / N
    ema = 0.95 * EMA0 + 0.05 * err_mag
    return np.minimum(err_mag / np.maximum(ema, 1e-8), 3.0)


def setup_inputs():
    s = mx_kscale(D)
    return {"x_pred": bf(np.random.standard_normal((N, D)) * s[None, :]),
            "W_gate": bf(np.random.standard_normal((H, D)) / np.sqrt(D) / s[None, :]),
            "W_up": bf(np.random.standard_normal((H, D)) / np.sqrt(D) / s[None, :]),
            "err": bf(np.random.standard_normal((N, D)) * 2.3)}


def reference(x_pred, W_gate, W_up, err):
    err = f64(err)
    sg = surprise_gate(err)
    xq = mxq(f64(x_pred), 1, "e4m3")
    gate_pre = xq @ mxq(f64(W_gate), 1, "e4m3").T
    up_pre = xq @ mxq(f64(W_up), 1, "e4m3").T
    h = silu(gate_pre) * up_pre
    grad_down = (mxq(err, 0, "e4m3").T @ mxq(h, 0, "e4m3")) / N
    return grad_down * sg

@@ -1,0 +1,246 @@
+from contextlib import ExitStack
+
+import concourse.mybir as mybir
+from concourse.masks import make_identity
+
+F32 = mybir.dt.float32
+BF16 = mybir.dt.bfloat16
+U32 = mybir.dt.uint32
+U8 = mybir.dt.uint8
+FP8X4 = mybir.dt.float8_e4m3fn_x4
+ACT = mybir.ActivationFunctionType
+ALU = mybir.AluOpType
+
+P = 128
+PACK = 4
+TOKENS = 8192
+FEATURES = 512
+HIDDEN = 128
+ROUND = P * PACK
+ROUNDS = TOKENS // ROUND
+WORDS = FEATURES // 2
+OUT_BLOCKS = FEATURES // P
+
+FLOPS = 2 * TOKENS * FEATURES * (2 * HIDDEN) + 2 * TOKENS * FEATURES * HIDDEN
+
+
+def tile_continuummemorysystem_pb_t_kernel(tc, x_pred, W_gate, W_up, err, out):
+    nc = tc.nc
+    with ExitStack() as ctx:
+        const = ctx.enter_context(tc.tile_pool(name="const", bufs=1))
+        raw = ctx.enter_context(tc.tile_pool(name="raw", bufs=ROUNDS))
+        work = ctx.enter_context(tc.tile_pool(name="work", bufs=3))
+        psum_t = ctx.enter_context(tc.psum_pool(name="psum_t", bufs=4))
+        psum_h = ctx.enter_context(tc.psum_pool(name="psum_h", bufs=1))
+        psum_acc = ctx.enter_context(tc.psum_pool(name="psum_acc", bufs=1))
+
+        w_raw = const.tile([P, 2, FEATURES], BF16)
+        nc.sync.dma_start(out=w_raw[:, 0, :], in_=W_gate)
+        nc.sync.dma_start(out=w_raw[:, 1, :], in_=W_up)
+        x_rounds = x_pred.rearrange("(c p j) k -> c p (j k)", p=P, j=PACK)
+        e_rounds = err.rearrange("(c p j) d -> c p j d", p=P, j=PACK)
+        x_raw = []
+        e_raw = []
+        for c in range(ROUNDS):
+            x_c = raw.tile([P, PACK * FEATURES], BF16, tag="x_raw")
+            nc.sync.dma_start(out=x_c[:], in_=x_rounds[c])
+            x_raw.append(x_c)
+            e_c = raw.tile([P, PACK, FEATURES], BF16, tag="e_raw")
+            nc.sync.dma_start(out=e_c[:], in_=e_rounds[c])
+            e_raw.append(e_c)
+
+        ident = const.tile([P, P], F32)
+        make_identity(nc, ident[:])
+        mean_matrix = const.tile([P, P], F32)
+        nc.vector.memset(mean_matrix[:], 1.0 / (TOKENS * TOKENS))
+        half = const.tile([P, 1], F32)
+        nc.vector.memset(half[:], 0.5)
+        square_sums = const.tile([P, ROUNDS], F32)
+
+        def transpose_words(bank, rows_words):
+            for u in range(2):
+                nc.tensor.transpose(bank[:, u, :], rows_words[:, u * P : (u + 1) * P], ident[:])
+
+        def interleaved(bank):
+            return bank.rearrange("p i u r -> p i r u")
+
+        w_bank = psum_t.tile([P, 2, 2, P], F32, tag="t")
+        for g in range(2):
+            transpose_words(w_bank[:, g], w_raw[:, g, :].bitcast(F32))
+        w_grouped = const.tile([P, 2 * HIDDEN * PACK], BF16, align_bytes=64)
+        nc.vector.tensor_copy(
+            out=w_grouped[:].bitcast(F32).rearrange("p (i r u) -> p i r u", i=2, u=2),
+            in_=interleaved(w_bank[:]),
+        )
+        w_codes = const.tile([P, 2 * HIDDEN], U32, align_bytes=64)
+        w_scales = const.tile([P, 2 * HIDDEN], U8, align_bytes=64)
+        nc.vector.quantize_mx(out=w_codes[:].bitcast(FP8X4), scales=w_scales[:], in_=w_grouped[:])
+
+        x_banks = {}
+        x_grouped = {}
+        x_quant = {}
+        e_grouped = {}
+        e_quant = {}
+        h_banks = {}
+        h_silu = {}
+        h_grouped = {}
+        h_quant = {}
+
+        def transpose_x(c):
+            words = x_raw[c][:].bitcast(F32)
+            for b in range(2):
+                bank = psum_t.tile([P, 2, 2, P], F32, tag="t")
+                for i in range(2):
+                    j = 2 * b + i
+                    transpose_words(bank[:, i], words[:, j * WORDS : (j + 1) * WORDS])
+                x_banks[c, b] = bank
+
+        def copy_x(c):
+            grouped = work.tile([P, ROUND * PACK], BF16, tag="x_grouped", align_bytes=64)
+            words = grouped[:].bitcast(F32).rearrange("p (b i r u) -> p b i r u", b=2, i=2, u=2)
+            nc.scalar.copy(out=words[:, 0], in_=interleaved(x_banks[c, 0][:]))
+            nc.vector.tensor_copy(out=words[:, 1], in_=interleaved(x_banks[c, 1][:]))
+            x_grouped[c] = grouped
+
+        def quantise_x(c):
+            codes = work.tile([P, ROUND], U32, tag="x_codes", align_bytes=64)
+            scales = work.tile([P, ROUND], U8, tag="x_scales", align_bytes=64)
+            nc.vector.quantize_mx(out=codes[:].bitcast(FP8X4), scales=scales[:], in_=x_grouped[c][:])
+            x_quant[c] = (codes, scales)
+
+        def first_products(c):
+            codes, scales = x_quant[c]
+            gate_bank = psum_h.tile([P, PACK, HIDDEN], F32, tag="gate")
+            up_bank = psum_h.tile([P, PACK, HIDDEN], F32, tag="up")
+            for g, bank in enumerate((gate_bank, up_bank)):
+                w_cols = slice(g * HIDDEN, (g + 1) * HIDDEN)
+                for j in range(PACK):
+                    m_cols = slice(j * P, (j + 1) * P)
+                    nc.tensor.matmul_mx(
+                        out=bank[:, j, :],
+                        lhsT=codes[:, m_cols].bitcast(FP8X4),
+                        lhsT_scale=scales[:, m_cols],
+                        rhs=w_codes[:, w_cols].bitcast(FP8X4),
+                        rhs_scale=w_scales[:, w_cols],
+                        start=True,
+                        stop=True,
+                    )
+            h_banks[c] = (gate_bank, up_bank)
+
+        def silu_gate(c):
+            silu = work.tile([P, PACK, HIDDEN], F32, tag="silu")
+            nc.scalar.activation(out=silu[:], in_=h_banks[c][0][:], func=ACT.Silu)
+            h_silu[c] = silu
+
+        def multiply_up(c):
+            grouped = work.tile([P, HIDDEN, PACK], BF16, tag="h_grouped", align_bytes=64)
+            nc.vector.tensor_tensor(
+                out=grouped[:],
+                in0=h_silu[c][:].rearrange("p j w -> p w j"),
+                in1=h_banks[c][1][:].rearrange("p j w -> p w j"),
+                op=ALU.mult,
+            )
+            h_grouped[c] = grouped
+
+        def quantise_h(c):
+            codes = work.tile([P, HIDDEN], U32, tag="h_codes", align_bytes=64)
+            scales = work.tile([P, HIDDEN], U8, tag="h_scales", align_bytes=64)
+            nc.vector.quantize_mx(
+                out=codes[:].bitcast(FP8X4), scales=scales[:], in_=h_grouped[c][:].rearrange("p w j -> p (w j)")
+            )
+            h_quant[c] = (codes, scales)
+
+        def group_err(c):
+            grouped = work.tile([P, FEATURES, PACK], BF16, tag="e_grouped", align_bytes=64)
+            nc.vector.tensor_copy(
+                out=grouped[:].rearrange("p (a i) j -> p a j i", i=4),
+                in_=e_raw[c][:].rearrange("p j (a i) -> p a j i", i=4),
+            )
+            e_grouped[c] = grouped
+
+        def quantise_err(c):
+            codes = work.tile([P, FEATURES], U32, tag="e_codes", align_bytes=64)
+            scales = work.tile([P, FEATURES], U8, tag="e_scales", align_bytes=64)
+            nc.vector.quantize_mx(
+                out=codes[:].bitcast(FP8X4), scales=scales[:], in_=e_grouped[c][:].rearrange("p d j -> p (d j)")
+            )
+            e_quant[c] = (codes, scales)
+
+        def square_err(c):
+            squares = work.tile([P, PACK, FEATURES], BF16, tag="squares")
+            nc.scalar.activation(
+                out=squares[:], in_=e_raw[c][:], func=ACT.Square, accum_out=square_sums[:, c : c + 1]
+            )
+
+        acc = psum_acc.tile([P, FEATURES], F32)
+
+        def second_product(c):
+            h_codes, h_scales = h_quant[c]
+            e_codes, e_scales = e_quant[c]
+            nc.tensor.matmul_mx(
+                out=acc[:],
+                lhsT=h_codes[:].bitcast(FP8X4),
+                lhsT_scale=h_scales[:],
+                rhs=e_codes[:].bitcast(FP8X4),
+                rhs_scale=e_scales[:],
+                start=(c == 0),
+                stop=(c == ROUNDS - 1),
+            )
+
+        def surprise_gate():
+            mean_bank = psum_t.tile([P, ROUNDS], F32, tag="t")
+            nc.tensor.matmul(out=mean_bank[:], lhsT=mean_matrix[:], rhs=square_sums[:], start=True, stop=True)
+            mag_squared = const.tile([P, 1], F32)
+            nc.vector.tensor_reduce(out=mag_squared[:], in_=mean_bank[:], axis=mybir.AxisListType.X, op=ALU.add)
+            err_mag = const.tile([P, 1], F32)
+            nc.gpsimd.tensor_tensor(out=err_mag[:], in0=mag_squared[:], in1=half[:], op=ALU.pow)
+            ema = const.tile([P, 1], F32)
+            nc.vector.tensor_scalar(out=ema[:], in0=err_mag[:], scalar1=0.05, scalar2=0.95, op0=ALU.mult, op1=ALU.add)
+            nc.vector.tensor_scalar_max(out=ema[:], in0=ema[:], scalar1=1e-8)
+            inverse = const.tile([P, 1], F32)
+            nc.vector.reciprocal(out=inverse[:], in_=ema[:])
+            ratio = const.tile([P, 1], F32)
+            nc.vector.tensor_tensor(out=ratio[:], in0=err_mag[:], in1=inverse[:], op=ALU.mult)
+            factor = const.tile([P, 1], F32)
+            nc.vector.tensor_scalar(
+                out=factor[:], in0=ratio[:], scalar1=3.0, scalar2=1.0 / TOKENS, op0=ALU.min, op1=ALU.mult
+            )
+            return factor
+
+        transpose_x(0)
+        copy_x(0)
+        transpose_x(1)
+        group_err(0)
+        square_err(0)
+        quantise_x(0)
+        first_products(0)
+        quantise_err(0)
+        factor = None
+        for c in range(ROUNDS):
+            following = c + 1 < ROUNDS
+            if c + 2 < ROUNDS:
+                transpose_x(c + 2)
+            if following:
+                copy_x(c + 1)
+            silu_gate(c)
+            if following:
+                group_err(c + 1)
+                quantise_x(c + 1)
+            else:
+                factor = surprise_gate()
+            multiply_up(c)
+            if following:
+                first_products(c + 1)
+                square_err(c + 1)
+                quantise_err(c + 1)
+            quantise_h(c)
+            second_product(c)
+
+        scaled = const.tile([P, FEATURES], F32)
+        nc.vector.tensor_scalar_mul(out=scaled[:], in0=acc[:], scalar1=factor[:, 0:1])
+        out_bank = psum_t.tile([P, OUT_BLOCKS, P], F32, tag="t")
+        for b in range(OUT_BLOCKS):
+            nc.tensor.transpose(out_bank[:, b, :], scaled[:, b * P : (b + 1) * P], ident[:])
+        result = const.tile([P, OUT_BLOCKS, HIDDEN], F32)
+        nc.vector.tensor_copy(out=result[:], in_=out_bank[:])
+        nc.sync.dma_start(out=out.rearrange("(b p) w -> p b w", p=P), in_=result[:])

@@ -20,6 +20,8 @@ ROUND = P * PACK
 ROUNDS = TOKENS // ROUND
 WORDS = FEATURES // 2
 OUT_BLOCKS = FEATURES // P
+GRAM_COLS = P
+VECTOR_COPY_EVERY = 4
 
 FLOPS = 2 * TOKENS * FEATURES * (2 * HIDDEN) + 2 * TOKENS * FEATURES * HIDDEN
 
@@ -30,24 +32,26 @@ def tile_continuummemorysystem_pb_t_kernel(tc, x_pred, W_gate, W_up, err, out):
         const = ctx.enter_context(tc.tile_pool(name="const", bufs=1))
         raw = ctx.enter_context(tc.tile_pool(name="raw", bufs=ROUNDS))
         work = ctx.enter_context(tc.tile_pool(name="work", bufs=3))
-        psum_t = ctx.enter_context(tc.psum_pool(name="psum_t", bufs=4))
-        psum_h = ctx.enter_context(tc.psum_pool(name="psum_h", bufs=1))
+        psum_t = ctx.enter_context(tc.psum_pool(name="psum_t", bufs=2))
+        psum_h = ctx.enter_context(tc.psum_pool(name="psum_h", bufs=2))
         psum_acc = ctx.enter_context(tc.psum_pool(name="psum_acc", bufs=1))
+        ctx.enter_context(tc.manual_schedule())
 
-        w_raw = const.tile([P, 2, FEATURES], BF16)
-        nc.sync.dma_start(out=w_raw[:, 0, :], in_=W_gate)
-        nc.sync.dma_start(out=w_raw[:, 1, :], in_=W_up)
         x_rounds = x_pred.rearrange("(c p j) k -> c p (j k)", p=P, j=PACK)
         e_rounds = err.rearrange("(c p j) d -> c p j d", p=P, j=PACK)
+        w_raw = const.tile([P, 2, FEATURES], BF16)
         x_raw = []
         e_raw = []
         for c in range(ROUNDS):
-            x_c = raw.tile([P, PACK * FEATURES], BF16, tag="x_raw")
-            nc.sync.dma_start(out=x_c[:], in_=x_rounds[c])
-            x_raw.append(x_c)
             e_c = raw.tile([P, PACK, FEATURES], BF16, tag="e_raw")
             nc.sync.dma_start(out=e_c[:], in_=e_rounds[c])
             e_raw.append(e_c)
+            if c == 0:
+                nc.sync.dma_start(out=w_raw[:, 0, :], in_=W_gate)
+                nc.sync.dma_start(out=w_raw[:, 1, :], in_=W_up)
+            x_c = raw.tile([P, PACK * FEATURES], BF16, tag="x_raw")
+            nc.sync.dma_start(out=x_c[:], in_=x_rounds[c])
+            x_raw.append(x_c)
 
         ident = const.tile([P, P], F32)
         make_identity(nc, ident[:])
@@ -55,7 +59,7 @@ def tile_continuummemorysystem_pb_t_kernel(tc, x_pred, W_gate, W_up, err, out):
         nc.vector.memset(mean_matrix[:], 1.0 / (TOKENS * TOKENS))
         half = const.tile([P, 1], F32)
         nc.vector.memset(half[:], 0.5)
-        square_sums = const.tile([P, ROUNDS], F32)
+        square_sums = const.tile([P, ROUNDS + GRAM_COLS], F32)
 
         def transpose_words(bank, rows_words):
             for u in range(2):
@@ -64,17 +68,19 @@ def tile_continuummemorysystem_pb_t_kernel(tc, x_pred, W_gate, W_up, err, out):
         def interleaved(bank):
             return bank.rearrange("p i u r -> p i r u")
 
-        w_bank = psum_t.tile([P, 2, 2, P], F32, tag="t")
-        for g in range(2):
-            transpose_words(w_bank[:, g], w_raw[:, g, :].bitcast(F32))
-        w_grouped = const.tile([P, 2 * HIDDEN * PACK], BF16, align_bytes=64)
-        nc.vector.tensor_copy(
-            out=w_grouped[:].bitcast(F32).rearrange("p (i r u) -> p i r u", i=2, u=2),
-            in_=interleaved(w_bank[:]),
-        )
         w_codes = const.tile([P, 2 * HIDDEN], U32, align_bytes=64)
         w_scales = const.tile([P, 2 * HIDDEN], U8, align_bytes=64)
-        nc.vector.quantize_mx(out=w_codes[:].bitcast(FP8X4), scales=w_scales[:], in_=w_grouped[:])
+
+        def quantise_weights():
+            w_bank = psum_t.tile([P, 2, 2, P], F32, tag="t")
+            for g in range(2):
+                transpose_words(w_bank[:, g], w_raw[:, g, :].bitcast(F32))
+            w_grouped = const.tile([P, 2 * HIDDEN * PACK], BF16, align_bytes=64)
+            nc.vector.tensor_copy(
+                out=w_grouped[:].bitcast(F32).rearrange("p (i r u) -> p i r u", i=2, u=2),
+                in_=interleaved(w_bank[:]),
+            )
+            nc.vector.quantize_mx(out=w_codes[:].bitcast(FP8X4), scales=w_scales[:], in_=w_grouped[:])
 
         x_banks = {}
         x_grouped = {}
@@ -99,7 +105,10 @@ def tile_continuummemorysystem_pb_t_kernel(tc, x_pred, W_gate, W_up, err, out):
             grouped = work.tile([P, ROUND * PACK], BF16, tag="x_grouped", align_bytes=64)
             words = grouped[:].bitcast(F32).rearrange("p (b i r u) -> p b i r u", b=2, i=2, u=2)
             nc.scalar.copy(out=words[:, 0], in_=interleaved(x_banks[c, 0][:]))
-            nc.vector.tensor_copy(out=words[:, 1], in_=interleaved(x_banks[c, 1][:]))
+            if c % VECTOR_COPY_EVERY == VECTOR_COPY_EVERY - 1:
+                nc.vector.tensor_copy(out=words[:, 1], in_=interleaved(x_banks[c, 1][:]))
+            else:
+                nc.scalar.copy(out=words[:, 1], in_=interleaved(x_banks[c, 1][:]))
             x_grouped[c] = grouped
 
         def quantise_x(c):
@@ -166,10 +175,24 @@ def tile_continuummemorysystem_pb_t_kernel(tc, x_pred, W_gate, W_up, err, out):
             )
             e_quant[c] = (codes, scales)
 
+        gram = psum_acc.tile([P, GRAM_COLS], F32)
+
         def square_err(c):
-            squares = work.tile([P, PACK, FEATURES], BF16, tag="squares")
+            for j in range(PACK):
+                block = e_raw[c][:, j, 0:GRAM_COLS]
+                nc.tensor.matmul(
+                    out=gram[:],
+                    lhsT=block,
+                    rhs=block,
+                    start=(c == 0 and j == 0),
+                    stop=(c == ROUNDS - 1 and j == PACK - 1),
+                )
+            squares = work.tile([P, PACK, FEATURES - GRAM_COLS], BF16, tag="squares")
             nc.scalar.activation(
-                out=squares[:], in_=e_raw[c][:], func=ACT.Square, accum_out=square_sums[:, c : c + 1]
+                out=squares[:],
+                in_=e_raw[c][:, :, GRAM_COLS:FEATURES],
+                func=ACT.Square,
+                accum_out=square_sums[:, c : c + 1],
             )
 
         acc = psum_acc.tile([P, FEATURES], F32)
@@ -187,13 +210,22 @@ def tile_continuummemorysystem_pb_t_kernel(tc, x_pred, W_gate, W_up, err, out):
                 stop=(c == ROUNDS - 1),
             )
 
-        def surprise_gate():
-            mean_bank = psum_t.tile([P, ROUNDS], F32, tag="t")
+        mean_banks = {}
+        err_mag = const.tile([P, 1], F32)
+        factor = const.tile([P, 1], F32)
+
+        def add_over_partitions():
+            nc.vector.tensor_tensor(out=square_sums[:, ROUNDS:], in0=gram[:], in1=ident[:], op=ALU.mult)
+            mean_bank = psum_t.tile([P, ROUNDS + GRAM_COLS], F32, tag="t")
             nc.tensor.matmul(out=mean_bank[:], lhsT=mean_matrix[:], rhs=square_sums[:], start=True, stop=True)
+            mean_banks[0] = mean_bank
+
+        def error_magnitude():
             mag_squared = const.tile([P, 1], F32)
-            nc.vector.tensor_reduce(out=mag_squared[:], in_=mean_bank[:], axis=mybir.AxisListType.X, op=ALU.add)
-            err_mag = const.tile([P, 1], F32)
+            nc.vector.tensor_reduce(out=mag_squared[:], in_=mean_banks[0][:], axis=mybir.AxisListType.X, op=ALU.add)
             nc.gpsimd.tensor_tensor(out=err_mag[:], in0=mag_squared[:], in1=half[:], op=ALU.pow)
+
+        def gate_factor():
             ema = const.tile([P, 1], F32)
             nc.vector.tensor_scalar(out=ema[:], in0=err_mag[:], scalar1=0.05, scalar2=0.95, op0=ALU.mult, op1=ALU.add)
             nc.vector.tensor_scalar_max(out=ema[:], in0=ema[:], scalar1=1e-8)
@@ -201,46 +233,50 @@ def tile_continuummemorysystem_pb_t_kernel(tc, x_pred, W_gate, W_up, err, out):
             nc.vector.reciprocal(out=inverse[:], in_=ema[:])
             ratio = const.tile([P, 1], F32)
             nc.vector.tensor_tensor(out=ratio[:], in0=err_mag[:], in1=inverse[:], op=ALU.mult)
-            factor = const.tile([P, 1], F32)
             nc.vector.tensor_scalar(
                 out=factor[:], in0=ratio[:], scalar1=3.0, scalar2=1.0 / TOKENS, op0=ALU.min, op1=ALU.mult
             )
-            return factor
 
-        transpose_x(0)
-        copy_x(0)
-        transpose_x(1)
         group_err(0)
         square_err(0)
-        quantise_x(0)
-        first_products(0)
+        quantise_weights()
+        transpose_x(0)
+        copy_x(0)
+        square_err(1)
         quantise_err(0)
-        factor = None
+        quantise_x(0)
+        transpose_x(1)
+        first_products(0)
         for c in range(ROUNDS):
-            following = c + 1 < ROUNDS
-            if c + 2 < ROUNDS:
-                transpose_x(c + 2)
-            if following:
+            one_ahead = c + 1 < ROUNDS
+            two_ahead = c + 2 < ROUNDS
+            if one_ahead:
                 copy_x(c + 1)
+            if two_ahead:
+                transpose_x(c + 2)
             silu_gate(c)
-            if following:
+            if one_ahead:
                 group_err(c + 1)
                 quantise_x(c + 1)
-            else:
-                factor = surprise_gate()
-            multiply_up(c)
-            if following:
                 first_products(c + 1)
-                square_err(c + 1)
+            multiply_up(c)
+            if two_ahead:
+                square_err(c + 2)
+            elif one_ahead:
+                add_over_partitions()
+            if one_ahead:
                 quantise_err(c + 1)
             quantise_h(c)
             second_product(c)
+            if one_ahead and not two_ahead:
+                error_magnitude()
+        gate_factor()
 
-        scaled = const.tile([P, FEATURES], F32)
-        nc.vector.tensor_scalar_mul(out=scaled[:], in0=acc[:], scalar1=factor[:, 0:1])
+        transposed = const.tile([P, FEATURES], F32)
+        nc.scalar.copy(out=transposed[:], in_=acc[:])
         out_bank = psum_t.tile([P, OUT_BLOCKS, P], F32, tag="t")
         for b in range(OUT_BLOCKS):
-            nc.tensor.transpose(out_bank[:, b, :], scaled[:, b * P : (b + 1) * P], ident[:])
+            nc.tensor.transpose(out_bank[:, b, :], transposed[:, b * P : (b + 1) * P], ident[:])
         result = const.tile([P, OUT_BLOCKS, HIDDEN], F32)
-        nc.vector.tensor_copy(out=result[:], in_=out_bank[:])
+        nc.vector.tensor_scalar_mul(out=result[:], in0=out_bank[:], scalar1=factor[:, 0:1])
         nc.sync.dma_start(out=out.rearrange("(b p) w -> p b w", p=P), in_=result[:])

@@ -42,16 +42,24 @@ def tile_continuummemorysystem_pb_t_kernel(tc, x_pred, W_gate, W_up, err, out):
         w_raw = const.tile([P, 2, FEATURES], BF16)
         x_raw = []
         e_raw = []
-        for c in range(ROUNDS):
+
+        def load_err(c):
             e_c = raw.tile([P, PACK, FEATURES], BF16, tag="e_raw")
             nc.sync.dma_start(out=e_c[:], in_=e_rounds[c])
             e_raw.append(e_c)
-            if c == 0:
-                nc.sync.dma_start(out=w_raw[:, 0, :], in_=W_gate)
-                nc.sync.dma_start(out=w_raw[:, 1, :], in_=W_up)
+
+        def load_x(c):
             x_c = raw.tile([P, PACK * FEATURES], BF16, tag="x_raw")
             nc.sync.dma_start(out=x_c[:], in_=x_rounds[c])
             x_raw.append(x_c)
+
+        load_err(0)
+        nc.sync.dma_start(out=w_raw[:, 0, :], in_=W_gate)
+        nc.sync.dma_start(out=w_raw[:, 1, :], in_=W_up)
+        load_x(0)
+        for c in range(1, ROUNDS):
+            load_x(c)
+            load_err(c)
 
         ident = const.tile([P, P], F32)
         make_identity(nc, ident[:])
@@ -242,34 +250,33 @@ def tile_continuummemorysystem_pb_t_kernel(tc, x_pred, W_gate, W_up, err, out):
         quantise_weights()
         transpose_x(0)
         copy_x(0)
-        square_err(1)
         quantise_err(0)
         quantise_x(0)
         transpose_x(1)
         first_products(0)
-        for c in range(ROUNDS):
-            one_ahead = c + 1 < ROUNDS
-            two_ahead = c + 2 < ROUNDS
-            if one_ahead:
-                copy_x(c + 1)
-            if two_ahead:
-                transpose_x(c + 2)
-            silu_gate(c)
-            if one_ahead:
-                group_err(c + 1)
-                quantise_x(c + 1)
-                first_products(c + 1)
-            multiply_up(c)
-            if two_ahead:
-                square_err(c + 2)
-            elif one_ahead:
+        for s in range(ROUNDS + 1):
+            if s + 1 < ROUNDS:
+                copy_x(s + 1)
+            if s + 2 < ROUNDS:
+                transpose_x(s + 2)
+            if s == ROUNDS - 1:
                 add_over_partitions()
-            if one_ahead:
-                quantise_err(c + 1)
-            quantise_h(c)
-            second_product(c)
-            if one_ahead and not two_ahead:
+            if s >= 1:
+                multiply_up(s - 1)
+            if s + 1 < ROUNDS:
+                square_err(s + 1)
+                group_err(s + 1)
+            if s == ROUNDS - 1:
                 error_magnitude()
+            if s >= 1:
+                quantise_h(s - 1)
+                second_product(s - 1)
+            if s + 1 < ROUNDS:
+                quantise_x(s + 1)
+                first_products(s + 1)
+                quantise_err(s + 1)
+            if s < ROUNDS:
+                silu_gate(s)
         gate_factor()
 
         transposed = const.tile([P, FEATURES], F32)

@@ -170,8 +170,8 @@ def tile_continuummemorysystem_pb_t_kernel(tc, x_pred, W_gate, W_up, err, out):
         def group_err(c):
             grouped = work.tile([P, FEATURES, PACK], BF16, tag="e_grouped", align_bytes=64)
             nc.vector.tensor_copy(
-                out=grouped[:].rearrange("p (a i) j -> p a j i", i=4),
-                in_=e_raw[c][:].rearrange("p j (a i) -> p a j i", i=4),
+                out=grouped[:].rearrange("p (a i) j -> p a j i", i=8),
+                in_=e_raw[c][:].rearrange("p j (a i) -> p a j i", i=8),
             )
             e_grouped[c] = grouped
 

@@ -145,15 +145,15 @@ def tile_continuummemorysystem_pb_t_kernel(tc, x_pred, W_gate, W_up, err, out):
             h_banks[c] = (gate_bank, up_bank)
 
         def silu_gate(c):
-            silu = work.tile([P, PACK, HIDDEN], F32, tag="silu")
-            nc.scalar.activation(out=silu[:], in_=h_banks[c][0][:], func=ACT.Silu)
+            silu = work.tile([P, HIDDEN, PACK], F32, tag="silu")
+            nc.scalar.activation(out=silu[:], in_=h_banks[c][0][:].rearrange("p j w -> p w j"), func=ACT.Silu)
             h_silu[c] = silu
 
         def multiply_up(c):
             grouped = work.tile([P, HIDDEN, PACK], BF16, tag="h_grouped", align_bytes=64)
             nc.vector.tensor_tensor(
                 out=grouped[:],
-                in0=h_silu[c][:].rearrange("p j w -> p w j"),
+                in0=h_silu[c][:],
                 in1=h_banks[c][1][:].rearrange("p j w -> p w j"),
                 op=ALU.mult,
             )

@@ -20,8 +20,10 @@ ROUND = P * PACK
 ROUNDS = TOKENS // ROUND
 WORDS = FEATURES // 2
 OUT_BLOCKS = FEATURES // P
+LATE = 2
 GRAM_COLS = P
-VECTOR_COPY_EVERY = 4
+FIVE_BLOCK_ROUNDS = 10
+ERR_LEAD = 2
 
 FLOPS = 2 * TOKENS * FEATURES * (2 * HIDDEN) + 2 * TOKENS * FEATURES * HIDDEN
 
@@ -32,6 +34,7 @@ def tile_continuummemorysystem_pb_t_kernel(tc, x_pred, W_gate, W_up, err, out):
         const = ctx.enter_context(tc.tile_pool(name="const", bufs=1))
         raw = ctx.enter_context(tc.tile_pool(name="raw", bufs=ROUNDS))
         work = ctx.enter_context(tc.tile_pool(name="work", bufs=3))
+        ready = ctx.enter_context(tc.tile_pool(name="ready", bufs=ERR_LEAD + 2))
         psum_t = ctx.enter_context(tc.psum_pool(name="psum_t", bufs=2))
         psum_h = ctx.enter_context(tc.psum_pool(name="psum_h", bufs=2))
         psum_acc = ctx.enter_context(tc.psum_pool(name="psum_acc", bufs=1))
@@ -58,8 +61,8 @@ def tile_continuummemorysystem_pb_t_kernel(tc, x_pred, W_gate, W_up, err, out):
         nc.sync.dma_start(out=w_raw[:, 1, :], in_=W_up)
         load_x(0)
         for c in range(1, ROUNDS):
-            load_x(c)
             load_err(c)
+            load_x(c)
 
         ident = const.tile([P, P], F32)
         make_identity(nc, ident[:])
@@ -79,16 +82,21 @@ def tile_continuummemorysystem_pb_t_kernel(tc, x_pred, W_gate, W_up, err, out):
         w_codes = const.tile([P, 2 * HIDDEN], U32, align_bytes=64)
         w_scales = const.tile([P, 2 * HIDDEN], U8, align_bytes=64)
 
-        def quantise_weights():
+        w_ready = []
+
+        def group_weights():
             w_bank = psum_t.tile([P, 2, 2, P], F32, tag="t")
             for g in range(2):
                 transpose_words(w_bank[:, g], w_raw[:, g, :].bitcast(F32))
             w_grouped = const.tile([P, 2 * HIDDEN * PACK], BF16, align_bytes=64)
-            nc.vector.tensor_copy(
+            nc.scalar.copy(
                 out=w_grouped[:].bitcast(F32).rearrange("p (i r u) -> p i r u", i=2, u=2),
                 in_=interleaved(w_bank[:]),
             )
-            nc.vector.quantize_mx(out=w_codes[:].bitcast(FP8X4), scales=w_scales[:], in_=w_grouped[:])
+            w_ready.append(w_grouped)
+
+        def quantise_weights():
+            nc.vector.quantize_mx(out=w_codes[:].bitcast(FP8X4), scales=w_scales[:], in_=w_ready[0][:])
 
         x_banks = {}
         x_grouped = {}
@@ -113,10 +121,7 @@ def tile_continuummemorysystem_pb_t_kernel(tc, x_pred, W_gate, W_up, err, out):
             grouped = work.tile([P, ROUND * PACK], BF16, tag="x_grouped", align_bytes=64)
             words = grouped[:].bitcast(F32).rearrange("p (b i r u) -> p b i r u", b=2, i=2, u=2)
             nc.scalar.copy(out=words[:, 0], in_=interleaved(x_banks[c, 0][:]))
-            if c % VECTOR_COPY_EVERY == VECTOR_COPY_EVERY - 1:
-                nc.vector.tensor_copy(out=words[:, 1], in_=interleaved(x_banks[c, 1][:]))
-            else:
-                nc.scalar.copy(out=words[:, 1], in_=interleaved(x_banks[c, 1][:]))
+            nc.scalar.copy(out=words[:, 1], in_=interleaved(x_banks[c, 1][:]))
             x_grouped[c] = grouped
 
         def quantise_x(c):
@@ -176,38 +181,60 @@ def tile_continuummemorysystem_pb_t_kernel(tc, x_pred, W_gate, W_up, err, out):
             e_grouped[c] = grouped
 
         def quantise_err(c):
-            codes = work.tile([P, FEATURES], U32, tag="e_codes", align_bytes=64)
-            scales = work.tile([P, FEATURES], U8, tag="e_scales", align_bytes=64)
+            codes = ready.tile([P, FEATURES], U32, tag="e_codes", align_bytes=64)
+            scales = ready.tile([P, FEATURES], U8, tag="e_scales", align_bytes=64)
             nc.vector.quantize_mx(
                 out=codes[:].bitcast(FP8X4), scales=scales[:], in_=e_grouped[c][:].rearrange("p d j -> p (d j)")
             )
             e_quant[c] = (codes, scales)
 
-        gram = psum_acc.tile([P, GRAM_COLS], F32)
+        gram = psum_acc.tile([P, GRAM_COLS], F32, tag="gram")
 
         def square_err(c):
-            for j in range(PACK):
-                block = e_raw[c][:, j, 0:GRAM_COLS]
+            values = e_raw[c][:].rearrange("p j d -> p (j d)")
+            blocks = 5 if c < FIVE_BLOCK_ROUNDS else 4
+            for k in range(blocks):
+                block = values[:, k * GRAM_COLS : (k + 1) * GRAM_COLS]
                 nc.tensor.matmul(
                     out=gram[:],
                     lhsT=block,
                     rhs=block,
-                    start=(c == 0 and j == 0),
-                    stop=(c == ROUNDS - 1 and j == PACK - 1),
+                    start=(c == 0 and k == 0),
+                    stop=(c == ROUNDS - 1 and k == blocks - 1),
                 )
-            squares = work.tile([P, PACK, FEATURES - GRAM_COLS], BF16, tag="squares")
+            squares = work.tile([P, PACK * FEATURES - 4 * GRAM_COLS], BF16, tag="squares")
+            rest = values[:, blocks * GRAM_COLS :]
             nc.scalar.activation(
-                out=squares[:],
-                in_=e_raw[c][:, :, GRAM_COLS:FEATURES],
+                out=squares[:, : PACK * FEATURES - blocks * GRAM_COLS],
+                in_=rest,
                 func=ACT.Square,
                 accum_out=square_sums[:, c : c + 1],
             )
 
-        acc = psum_acc.tile([P, FEATURES], F32)
+        acc = psum_acc.tile([P, FEATURES], F32, tag="acc")
+        late_banks = []
 
         def second_product(c):
             h_codes, h_scales = h_quant[c]
             e_codes, e_scales = e_quant[c]
+            if c >= ROUNDS - LATE:
+                if not late_banks:
+                    late_banks.append(psum_t.tile([P, HIDDEN], F32, tag="t", name="late_0"))
+                    late_banks.append(psum_t.tile([P, HIDDEN], F32, tag="t", name="late_1"))
+                    late_banks.append(psum_h.tile([P, HIDDEN], F32, tag="gate", name="late_2"))
+                    late_banks.append(psum_h.tile([P, HIDDEN], F32, tag="up", name="late_3"))
+                for b, bank in enumerate(late_banks):
+                    f_cols = slice(b * P, (b + 1) * P)
+                    nc.tensor.matmul_mx(
+                        out=bank[:],
+                        lhsT=e_codes[:, f_cols].bitcast(FP8X4),
+                        lhsT_scale=e_scales[:, f_cols],
+                        rhs=h_codes[:].bitcast(FP8X4),
+                        rhs_scale=h_scales[:],
+                        start=(c == ROUNDS - LATE),
+                        stop=(c == ROUNDS - 1),
+                    )
+                return
             nc.tensor.matmul_mx(
                 out=acc[:],
                 lhsT=h_codes[:].bitcast(FP8X4),
@@ -215,16 +242,18 @@ def tile_continuummemorysystem_pb_t_kernel(tc, x_pred, W_gate, W_up, err, out):
                 rhs=e_codes[:].bitcast(FP8X4),
                 rhs_scale=e_scales[:],
                 start=(c == 0),
-                stop=(c == ROUNDS - 1),
+                stop=(c == ROUNDS - LATE - 1),
             )
 
         mean_banks = {}
         err_mag = const.tile([P, 1], F32)
+        ema = const.tile([P, 1], F32)
+        floored = const.tile([P, 1], F32)
         factor = const.tile([P, 1], F32)
 
         def add_over_partitions():
             nc.vector.tensor_tensor(out=square_sums[:, ROUNDS:], in0=gram[:], in1=ident[:], op=ALU.mult)
-            mean_bank = psum_t.tile([P, ROUNDS + GRAM_COLS], F32, tag="t")
+            mean_bank = psum_acc.tile([P, ROUNDS + GRAM_COLS], F32, tag="gram")
             nc.tensor.matmul(out=mean_bank[:], lhsT=mean_matrix[:], rhs=square_sums[:], start=True, stop=True)
             mean_banks[0] = mean_bank
 
@@ -232,58 +261,87 @@ def tile_continuummemorysystem_pb_t_kernel(tc, x_pred, W_gate, W_up, err, out):
             mag_squared = const.tile([P, 1], F32)
             nc.vector.tensor_reduce(out=mag_squared[:], in_=mean_banks[0][:], axis=mybir.AxisListType.X, op=ALU.add)
             nc.gpsimd.tensor_tensor(out=err_mag[:], in0=mag_squared[:], in1=half[:], op=ALU.pow)
+            nc.gpsimd.tensor_scalar(out=ema[:], in0=err_mag[:], scalar1=0.05, scalar2=0.95, op0=ALU.mult, op1=ALU.add)
+            nc.gpsimd.tensor_scalar(out=floored[:], in0=ema[:], scalar1=1e-8, scalar2=None, op0=ALU.max)
 
         def gate_factor():
-            ema = const.tile([P, 1], F32)
-            nc.vector.tensor_scalar(out=ema[:], in0=err_mag[:], scalar1=0.05, scalar2=0.95, op0=ALU.mult, op1=ALU.add)
-            nc.vector.tensor_scalar_max(out=ema[:], in0=ema[:], scalar1=1e-8)
             inverse = const.tile([P, 1], F32)
-            nc.vector.reciprocal(out=inverse[:], in_=ema[:])
+            nc.vector.reciprocal(out=inverse[:], in_=floored[:])
             ratio = const.tile([P, 1], F32)
-            nc.vector.tensor_tensor(out=ratio[:], in0=err_mag[:], in1=inverse[:], op=ALU.mult)
-            nc.vector.tensor_scalar(
+            nc.gpsimd.tensor_tensor(out=ratio[:], in0=err_mag[:], in1=inverse[:], op=ALU.mult)
+            nc.gpsimd.tensor_scalar(
                 out=factor[:], in0=ratio[:], scalar1=3.0, scalar2=1.0 / TOKENS, op0=ALU.min, op1=ALU.mult
             )
 
+        transposed = const.tile([P, FEATURES], F32)
+        early_banks = []
+        early = const.tile([P, OUT_BLOCKS, HIDDEN], F32)
+
+        def copy_early():
+            nc.scalar.copy(out=transposed[:], in_=acc[:])
+
+        def transpose_early():
+            bank = psum_acc.tile([P, OUT_BLOCKS, P], F32, tag="acc", name="early_bank")
+            for b in range(OUT_BLOCKS):
+                nc.tensor.transpose(bank[:, b, :], transposed[:, b * P : (b + 1) * P], ident[:])
+            early_banks.append(bank)
+
+        def scale_early():
+            nc.scalar.activation(out=early[:], in_=early_banks[0][:], func=ACT.Copy, scale=factor[:, 0:1])
+
         group_err(0)
         square_err(0)
-        quantise_weights()
+        group_weights()
         transpose_x(0)
-        copy_x(0)
         quantise_err(0)
+        quantise_weights()
+        group_err(1)
+        copy_x(0)
         quantise_x(0)
         transpose_x(1)
         first_products(0)
-        for s in range(ROUNDS + 1):
+        quantise_err(1)
+        square_err(1)
+        for s in range(ROUNDS):
+            ahead = s + ERR_LEAD
             if s + 1 < ROUNDS:
                 copy_x(s + 1)
+            if ahead < ROUNDS:
+                group_err(ahead)
             if s + 2 < ROUNDS:
                 transpose_x(s + 2)
-            if s == ROUNDS - 1:
-                add_over_partitions()
-            if s >= 1:
-                multiply_up(s - 1)
-            if s + 1 < ROUNDS:
-                square_err(s + 1)
-                group_err(s + 1)
-            if s == ROUNDS - 1:
-                error_magnitude()
-            if s >= 1:
-                quantise_h(s - 1)
-                second_product(s - 1)
+            silu_gate(s)
             if s + 1 < ROUNDS:
                 quantise_x(s + 1)
+            multiply_up(s)
+            if s + 1 < ROUNDS:
                 first_products(s + 1)
-                quantise_err(s + 1)
-            if s < ROUNDS:
-                silu_gate(s)
-        gate_factor()
+            if ahead < ROUNDS:
+                quantise_err(ahead)
+                square_err(ahead)
+            elif s < ROUNDS - 1:
+                error_magnitude()
+            else:
+                gate_factor()
+            quantise_h(s)
+            second_product(s)
+            if ahead == ROUNDS - 1:
+                add_over_partitions()
+            if s == ROUNDS - LATE:
+                copy_early()
+                transpose_early()
+        scale_early()
 
-        transposed = const.tile([P, FEATURES], F32)
-        nc.scalar.copy(out=transposed[:], in_=acc[:])
-        out_bank = psum_t.tile([P, OUT_BLOCKS, P], F32, tag="t")
-        for b in range(OUT_BLOCKS):
-            nc.tensor.transpose(out_bank[:, b, :], transposed[:, b * P : (b + 1) * P], ident[:])
         result = const.tile([P, OUT_BLOCKS, HIDDEN], F32)
-        nc.vector.tensor_scalar_mul(out=result[:], in0=out_bank[:], scalar1=factor[:, 0:1])
-        nc.sync.dma_start(out=out.rearrange("(b p) w -> p b w", p=P), in_=result[:])
+        out_blocks = out.rearrange("(b p) w -> p b w", p=P)
+        for b in range(OUT_BLOCKS):
+            nc.vector.scalar_tensor_tensor(
+                out=result[:, b, :],
+                in0=late_banks[b][:],
+                scalar=factor[:, 0:1],
+                in1=early[:, b, :],
+                op0=ALU.mult,
+                op1=ALU.add,
+            )
+            if b % 2 == 1:
+                nc.sync.dma_start(out=out_blocks[:, b - 1 : b + 1, :], in_=result[:, b - 1 : b + 1, :])

@@ -23,6 +23,7 @@ OUT_BLOCKS = FEATURES // P
 LATE = 2
 GRAM_COLS = P
 FIVE_BLOCK_ROUNDS = 10
+VECTOR_COPY_EVERY = 4
 ERR_LEAD = 2
 
 FLOPS = 2 * TOKENS * FEATURES * (2 * HIDDEN) + 2 * TOKENS * FEATURES * HIDDEN
@@ -121,7 +122,10 @@ def tile_continuummemorysystem_pb_t_kernel(tc, x_pred, W_gate, W_up, err, out):
             grouped = work.tile([P, ROUND * PACK], BF16, tag="x_grouped", align_bytes=64)
             words = grouped[:].bitcast(F32).rearrange("p (b i r u) -> p b i r u", b=2, i=2, u=2)
             nc.scalar.copy(out=words[:, 0], in_=interleaved(x_banks[c, 0][:]))
-            nc.scalar.copy(out=words[:, 1], in_=interleaved(x_banks[c, 1][:]))
+            if c % VECTOR_COPY_EVERY == VECTOR_COPY_EVERY - 1:
+                nc.vector.tensor_copy(out=words[:, 1], in_=interleaved(x_banks[c, 1][:]))
+            else:
+                nc.scalar.copy(out=words[:, 1], in_=interleaved(x_banks[c, 1][:]))
             x_grouped[c] = grouped
 
         def quantise_x(c):

@@ -23,7 +23,7 @@ OUT_BLOCKS = FEATURES // P
 LATE = 2
 GRAM_COLS = P
 FIVE_BLOCK_ROUNDS = 10
-VECTOR_COPY_EVERY = 4
+VECTOR_COPY_EVERY = 6
 ERR_LEAD = 2
 
 FLOPS = 2 * TOKENS * FEATURES * (2 * HIDDEN) + 2 * TOKENS * FEATURES * HIDDEN
@@ -83,21 +83,24 @@ def tile_continuummemorysystem_pb_t_kernel(tc, x_pred, W_gate, W_up, err, out):
         w_codes = const.tile([P, 2 * HIDDEN], U32, align_bytes=64)
         w_scales = const.tile([P, 2 * HIDDEN], U8, align_bytes=64)
 
-        w_ready = []
+        w_banks = []
 
-        def group_weights():
-            w_bank = psum_t.tile([P, 2, 2, P], F32, tag="t")
+        def transpose_weights():
+            w_bank = psum_h.tile([P, 2, 2, P], F32, tag="gate", name="w_bank")
             for g in range(2):
                 transpose_words(w_bank[:, g], w_raw[:, g, :].bitcast(F32))
-            w_grouped = const.tile([P, 2 * HIDDEN * PACK], BF16, align_bytes=64)
+            w_banks.append(w_bank)
+
+        w_grouped = const.tile([P, 2 * HIDDEN * PACK], BF16, align_bytes=64)
+
+        def copy_weights():
             nc.scalar.copy(
                 out=w_grouped[:].bitcast(F32).rearrange("p (i r u) -> p i r u", i=2, u=2),
-                in_=interleaved(w_bank[:]),
+                in_=interleaved(w_banks[0][:]),
             )
-            w_ready.append(w_grouped)
 
         def quantise_weights():
-            nc.vector.quantize_mx(out=w_codes[:].bitcast(FP8X4), scales=w_scales[:], in_=w_ready[0][:])
+            nc.vector.quantize_mx(out=w_codes[:].bitcast(FP8X4), scales=w_scales[:], in_=w_grouped[:])
 
         x_banks = {}
         x_grouped = {}
@@ -122,7 +125,7 @@ def tile_continuummemorysystem_pb_t_kernel(tc, x_pred, W_gate, W_up, err, out):
             grouped = work.tile([P, ROUND * PACK], BF16, tag="x_grouped", align_bytes=64)
             words = grouped[:].bitcast(F32).rearrange("p (b i r u) -> p b i r u", b=2, i=2, u=2)
             nc.scalar.copy(out=words[:, 0], in_=interleaved(x_banks[c, 0][:]))
-            if c % VECTOR_COPY_EVERY == VECTOR_COPY_EVERY - 1:
+            if c > 0 and c % VECTOR_COPY_EVERY == 0:
                 nc.vector.tensor_copy(out=words[:, 1], in_=interleaved(x_banks[c, 1][:]))
             else:
                 nc.scalar.copy(out=words[:, 1], in_=interleaved(x_banks[c, 1][:]))
@@ -194,9 +197,12 @@ def tile_continuummemorysystem_pb_t_kernel(tc, x_pred, W_gate, W_up, err, out):
 
         gram = psum_acc.tile([P, GRAM_COLS], F32, tag="gram")
 
-        def square_err(c):
+        def gram_blocks(c):
+            return 5 if c < FIVE_BLOCK_ROUNDS else 4
+
+        def gram_err(c):
             values = e_raw[c][:].rearrange("p j d -> p (j d)")
-            blocks = 5 if c < FIVE_BLOCK_ROUNDS else 4
+            blocks = gram_blocks(c)
             for k in range(blocks):
                 block = values[:, k * GRAM_COLS : (k + 1) * GRAM_COLS]
                 nc.tensor.matmul(
@@ -206,11 +212,13 @@ def tile_continuummemorysystem_pb_t_kernel(tc, x_pred, W_gate, W_up, err, out):
                     start=(c == 0 and k == 0),
                     stop=(c == ROUNDS - 1 and k == blocks - 1),
                 )
+
+        def square_err(c):
+            first = gram_blocks(c) * GRAM_COLS
             squares = work.tile([P, PACK * FEATURES - 4 * GRAM_COLS], BF16, tag="squares")
-            rest = values[:, blocks * GRAM_COLS :]
             nc.scalar.activation(
-                out=squares[:, : PACK * FEATURES - blocks * GRAM_COLS],
-                in_=rest,
+                out=squares[:, : PACK * FEATURES - first],
+                in_=e_raw[c][:].rearrange("p j d -> p (j d)")[:, first:],
                 func=ACT.Square,
                 accum_out=square_sums[:, c : c + 1],
             )
@@ -255,8 +263,10 @@ def tile_continuummemorysystem_pb_t_kernel(tc, x_pred, W_gate, W_up, err, out):
         floored = const.tile([P, 1], F32)
         factor = const.tile([P, 1], F32)
 
-        def add_over_partitions():
+        def pick_diagonal():
             nc.vector.tensor_tensor(out=square_sums[:, ROUNDS:], in0=gram[:], in1=ident[:], op=ALU.mult)
+
+        def add_over_partitions():
             mean_bank = psum_acc.tile([P, ROUNDS + GRAM_COLS], F32, tag="gram")
             nc.tensor.matmul(out=mean_bank[:], lhsT=mean_matrix[:], rhs=square_sums[:], start=True, stop=True)
             mean_banks[0] = mean_bank
@@ -294,17 +304,20 @@ def tile_continuummemorysystem_pb_t_kernel(tc, x_pred, W_gate, W_up, err, out):
             nc.scalar.activation(out=early[:], in_=early_banks[0][:], func=ACT.Copy, scale=factor[:, 0:1])
 
         group_err(0)
+        gram_err(0)
         square_err(0)
-        group_weights()
+        transpose_weights()
         transpose_x(0)
+        copy_weights()
         quantise_err(0)
+        copy_x(0)
+        transpose_x(1)
         quantise_weights()
         group_err(1)
-        copy_x(0)
         quantise_x(0)
-        transpose_x(1)
         first_products(0)
         quantise_err(1)
+        gram_err(1)
         square_err(1)
         for s in range(ROUNDS):
             ahead = s + ERR_LEAD
@@ -315,8 +328,12 @@ def tile_continuummemorysystem_pb_t_kernel(tc, x_pred, W_gate, W_up, err, out):
             if s + 2 < ROUNDS:
                 transpose_x(s + 2)
             silu_gate(s)
+            if ahead < ROUNDS:
+                gram_err(ahead)
             if s + 1 < ROUNDS:
                 quantise_x(s + 1)
+            if ahead == ROUNDS - 1:
+                pick_diagonal()
             multiply_up(s)
             if s + 1 < ROUNDS:
                 first_products(s + 1)

@@ -71,6 +71,8 @@ def tile_continuummemorysystem_pb_t_kernel(tc, x_pred, W_gate, W_up, err, out):
         nc.vector.memset(mean_matrix[:], 1.0 / (TOKENS * TOKENS))
         half = const.tile([P, 1], F32)
         nc.vector.memset(half[:], 0.5)
+        table_load = const.tile([P, 1], F32)
+        nc.scalar.activation(out=table_load[:], in_=half[:], func=ACT.Silu)
         square_sums = const.tile([P, ROUNDS + GRAM_COLS], F32)
 
         def transpose_words(bank, rows_words):

@@ -22,7 +22,7 @@ WORDS = FEATURES // 2
 OUT_BLOCKS = FEATURES // P
 LATE = 2
 GRAM_COLS = P
-FIVE_BLOCK_ROUNDS = 10
+FIVE_BLOCK_ROUNDS = 11
 VECTOR_COPY_EVERY = 6
 ERR_LEAD = 2
 
@@ -133,19 +133,30 @@ def tile_continuummemorysystem_pb_t_kernel(tc, x_pred, W_gate, W_up, err, out):
                 nc.scalar.copy(out=words[:, 1], in_=interleaved(x_banks[c, 1][:]))
             x_grouped[c] = grouped
 
-        def quantise_x(c):
-            codes = work.tile([P, ROUND], U32, tag="x_codes", align_bytes=64)
-            scales = work.tile([P, ROUND], U8, tag="x_scales", align_bytes=64)
-            nc.vector.quantize_mx(out=codes[:].bitcast(FP8X4), scales=scales[:], in_=x_grouped[c][:])
-            x_quant[c] = (codes, scales)
-
-        def first_products(c):
+        def quantise_x(c, part, parts):
+            if part == 0:
+                codes = work.tile([P, ROUND], U32, tag="x_codes", align_bytes=64)
+                scales = work.tile([P, ROUND], U8, tag="x_scales", align_bytes=64)
+                x_quant[c] = (codes, scales)
             codes, scales = x_quant[c]
-            gate_bank = psum_h.tile([P, PACK, HIDDEN], F32, tag="gate")
-            up_bank = psum_h.tile([P, PACK, HIDDEN], F32, tag="up")
-            for g, bank in enumerate((gate_bank, up_bank)):
+            width = ROUND // parts
+            cols = slice(part * width, (part + 1) * width)
+            nc.vector.quantize_mx(
+                out=codes[:, cols].bitcast(FP8X4),
+                scales=scales[:, cols],
+                in_=x_grouped[c][:, part * width * PACK : (part + 1) * width * PACK],
+            )
+
+        def first_products(c, part, parts):
+            codes, scales = x_quant[c]
+            if part == 0:
+                gate_bank = psum_h.tile([P, PACK, HIDDEN], F32, tag="gate")
+                up_bank = psum_h.tile([P, PACK, HIDDEN], F32, tag="up")
+                h_banks[c] = (gate_bank, up_bank)
+            for g in (0, 1):
+                bank = h_banks[c][g]
                 w_cols = slice(g * HIDDEN, (g + 1) * HIDDEN)
-                for j in range(PACK):
+                for j in range(part * PACK // parts, (part + 1) * PACK // parts):
                     m_cols = slice(j * P, (j + 1) * P)
                     nc.tensor.matmul_mx(
                         out=bank[:, j, :],
@@ -156,7 +167,6 @@ def tile_continuummemorysystem_pb_t_kernel(tc, x_pred, W_gate, W_up, err, out):
                         start=True,
                         stop=True,
                     )
-            h_banks[c] = (gate_bank, up_bank)
 
         def silu_gate(c):
             silu = work.tile([P, HIDDEN, PACK], F32, tag="silu")
@@ -316,8 +326,8 @@ def tile_continuummemorysystem_pb_t_kernel(tc, x_pred, W_gate, W_up, err, out):
         transpose_x(1)
         quantise_weights()
         group_err(1)
-        quantise_x(0)
-        first_products(0)
+        quantise_x(0, 0, 1)
+        first_products(0, 0, 1)
         quantise_err(1)
         gram_err(1)
         square_err(1)
@@ -333,26 +343,27 @@ def tile_continuummemorysystem_pb_t_kernel(tc, x_pred, W_gate, W_up, err, out):
             if ahead < ROUNDS:
                 gram_err(ahead)
             if s + 1 < ROUNDS:
-                quantise_x(s + 1)
+                parts = 2 if s + 1 == ROUNDS - 1 else 1
+                for part in range(parts):
+                    quantise_x(s + 1, part, parts)
+                    first_products(s + 1, part, parts)
             if ahead == ROUNDS - 1:
                 pick_diagonal()
+            if s == ROUNDS - 2:
+                error_magnitude()
             multiply_up(s)
-            if s + 1 < ROUNDS:
-                first_products(s + 1)
             if ahead < ROUNDS:
                 quantise_err(ahead)
                 square_err(ahead)
-            elif s < ROUNDS - 1:
-                error_magnitude()
-            else:
+            if s == ROUNDS - 2:
                 gate_factor()
-            quantise_h(s)
-            second_product(s)
             if ahead == ROUNDS - 1:
                 add_over_partitions()
             if s == ROUNDS - LATE:
                 copy_early()
                 transpose_early()
+            quantise_h(s)
+            second_product(s)
         scale_early()
 
         result = const.tile([P, OUT_BLOCKS, HIDDEN], F32)

@@ -133,7 +133,11 @@ def tile_continuummemorysystem_pb_t_kernel(tc, x_pred, W_gate, W_up, err, out):
                 nc.scalar.copy(out=words[:, 1], in_=interleaved(x_banks[c, 1][:]))
             x_grouped[c] = grouped
 
-        def quantise_x(c, part, parts):
+        def parts_of(c):
+            return 2 if c == ROUNDS - 1 else 1
+
+        def quantise_x(c, part):
+            parts = parts_of(c)
             if part == 0:
                 codes = work.tile([P, ROUND], U32, tag="x_codes", align_bytes=64)
                 scales = work.tile([P, ROUND], U8, tag="x_scales", align_bytes=64)
@@ -147,7 +151,8 @@ def tile_continuummemorysystem_pb_t_kernel(tc, x_pred, W_gate, W_up, err, out):
                 in_=x_grouped[c][:, part * width * PACK : (part + 1) * width * PACK],
             )
 
-        def first_products(c, part, parts):
+        def first_products(c, part):
+            parts = parts_of(c)
             codes, scales = x_quant[c]
             if part == 0:
                 gate_bank = psum_h.tile([P, PACK, HIDDEN], F32, tag="gate")
@@ -168,27 +173,41 @@ def tile_continuummemorysystem_pb_t_kernel(tc, x_pred, W_gate, W_up, err, out):
                         stop=True,
                     )
 
+        def hidden_part(c, part):
+            width = HIDDEN // parts_of(c)
+            return slice(part * width, (part + 1) * width)
+
         def silu_gate(c):
             silu = work.tile([P, HIDDEN, PACK], F32, tag="silu")
-            nc.scalar.activation(out=silu[:], in_=h_banks[c][0][:].rearrange("p j w -> p w j"), func=ACT.Silu)
+            for part in range(parts_of(c)):
+                w = hidden_part(c, part)
+                nc.scalar.activation(
+                    out=silu[:, w, :], in_=h_banks[c][0][:, :, w].rearrange("p j w -> p w j"), func=ACT.Silu
+                )
             h_silu[c] = silu
 
         def multiply_up(c):
             grouped = work.tile([P, HIDDEN, PACK], BF16, tag="h_grouped", align_bytes=64)
-            nc.vector.tensor_tensor(
-                out=grouped[:],
-                in0=h_silu[c][:],
-                in1=h_banks[c][1][:].rearrange("p j w -> p w j"),
-                op=ALU.mult,
-            )
+            for part in range(parts_of(c)):
+                w = hidden_part(c, part)
+                nc.vector.tensor_tensor(
+                    out=grouped[:, w, :],
+                    in0=h_silu[c][:, w, :],
+                    in1=h_banks[c][1][:, :, w].rearrange("p j w -> p w j"),
+                    op=ALU.mult,
+                )
             h_grouped[c] = grouped
 
         def quantise_h(c):
             codes = work.tile([P, HIDDEN], U32, tag="h_codes", align_bytes=64)
             scales = work.tile([P, HIDDEN], U8, tag="h_scales", align_bytes=64)
-            nc.vector.quantize_mx(
-                out=codes[:].bitcast(FP8X4), scales=scales[:], in_=h_grouped[c][:].rearrange("p w j -> p (w j)")
-            )
+            for part in range(parts_of(c)):
+                w = hidden_part(c, part)
+                nc.vector.quantize_mx(
+                    out=codes[:, w].bitcast(FP8X4),
+                    scales=scales[:, w],
+                    in_=h_grouped[c][:, w, :].rearrange("p w j -> p (w j)"),
+                )
             h_quant[c] = (codes, scales)
 
         def group_err(c):
@@ -272,7 +291,6 @@ def tile_continuummemorysystem_pb_t_kernel(tc, x_pred, W_gate, W_up, err, out):
         mean_banks = {}
         err_mag = const.tile([P, 1], F32)
         ema = const.tile([P, 1], F32)
-        floored = const.tile([P, 1], F32)
         factor = const.tile([P, 1], F32)
 
         def pick_diagonal():
@@ -287,16 +305,15 @@ def tile_continuummemorysystem_pb_t_kernel(tc, x_pred, W_gate, W_up, err, out):
             mag_squared = const.tile([P, 1], F32)
             nc.vector.tensor_reduce(out=mag_squared[:], in_=mean_banks[0][:], axis=mybir.AxisListType.X, op=ALU.add)
             nc.gpsimd.tensor_tensor(out=err_mag[:], in0=mag_squared[:], in1=half[:], op=ALU.pow)
-            nc.gpsimd.tensor_scalar(out=ema[:], in0=err_mag[:], scalar1=0.05, scalar2=0.95, op0=ALU.mult, op1=ALU.add)
-            nc.gpsimd.tensor_scalar(out=floored[:], in0=ema[:], scalar1=1e-8, scalar2=None, op0=ALU.max)
+            nc.gpsimd.tensor_scalar(
+                out=ema[:], in0=err_mag[:], scalar1=0.05 * TOKENS, scalar2=0.95 * TOKENS, op0=ALU.mult, op1=ALU.add
+            )
 
         def gate_factor():
             inverse = const.tile([P, 1], F32)
-            nc.vector.reciprocal(out=inverse[:], in_=floored[:])
-            ratio = const.tile([P, 1], F32)
-            nc.gpsimd.tensor_tensor(out=ratio[:], in0=err_mag[:], in1=inverse[:], op=ALU.mult)
+            nc.vector.reciprocal(out=inverse[:], in_=ema[:])
             nc.gpsimd.tensor_scalar(
-                out=factor[:], in0=ratio[:], scalar1=3.0, scalar2=1.0 / TOKENS, op0=ALU.min, op1=ALU.mult
+                out=factor[:], in0=err_mag[:], scalar1=inverse[:, 0:1], scalar2=3.0 / TOKENS, op0=ALU.mult, op1=ALU.min
             )
 
         transposed = const.tile([P, FEATURES], F32)
@@ -313,7 +330,10 @@ def tile_continuummemorysystem_pb_t_kernel(tc, x_pred, W_gate, W_up, err, out):
             early_banks.append(bank)
 
         def scale_early():
-            nc.scalar.activation(out=early[:], in_=early_banks[0][:], func=ACT.Copy, scale=factor[:, 0:1])
+            for b in (0, 2):
+                nc.scalar.activation(
+                    out=early[:, b : b + 2, :], in_=early_banks[0][:, b : b + 2, :], func=ACT.Copy, scale=factor[:, 0:1]
+                )
 
         group_err(0)
         gram_err(0)
@@ -326,8 +346,8 @@ def tile_continuummemorysystem_pb_t_kernel(tc, x_pred, W_gate, W_up, err, out):
         transpose_x(1)
         quantise_weights()
         group_err(1)
-        quantise_x(0, 0, 1)
-        first_products(0, 0, 1)
+        quantise_x(0, 0)
+        first_products(0, 0)
         quantise_err(1)
         gram_err(1)
         square_err(1)
@@ -343,10 +363,9 @@ def tile_continuummemorysystem_pb_t_kernel(tc, x_pred, W_gate, W_up, err, out):
             if ahead < ROUNDS:
                 gram_err(ahead)
             if s + 1 < ROUNDS:
-                parts = 2 if s + 1 == ROUNDS - 1 else 1
-                for part in range(parts):
-                    quantise_x(s + 1, part, parts)
-                    first_products(s + 1, part, parts)
+                for part in range(parts_of(s + 1)):
+                    quantise_x(s + 1, part)
+                    first_products(s + 1, part)
             if ahead == ROUNDS - 1:
                 pick_diagonal()
             if s == ROUNDS - 2:

from contextlib import ExitStack

import concourse.mybir as mybir
from concourse.masks import make_identity

F32 = mybir.dt.float32
BF16 = mybir.dt.bfloat16
U32 = mybir.dt.uint32
U8 = mybir.dt.uint8
FP8X4 = mybir.dt.float8_e4m3fn_x4
ACT = mybir.ActivationFunctionType
ALU = mybir.AluOpType

P = 128
PACK = 4
TOKENS = 8192
FEATURES = 512
HIDDEN = 128
ROUND = P * PACK
ROUNDS = TOKENS // ROUND
WORDS = FEATURES // 2
OUT_BLOCKS = FEATURES // P
LATE = 2
GRAM_COLS = P
FIVE_BLOCK_ROUNDS = 11
VECTOR_COPY_EVERY = 6
ERR_LEAD = 2

FLOPS = 2 * TOKENS * FEATURES * (2 * HIDDEN) + 2 * TOKENS * FEATURES * HIDDEN


def tile_continuummemorysystem_pb_t_kernel(tc, x_pred, W_gate, W_up, err, out):
    nc = tc.nc
    with ExitStack() as ctx:
        const = ctx.enter_context(tc.tile_pool(name="const", bufs=1))
        raw = ctx.enter_context(tc.tile_pool(name="raw", bufs=ROUNDS))
        work = ctx.enter_context(tc.tile_pool(name="work", bufs=3))
        ready = ctx.enter_context(tc.tile_pool(name="ready", bufs=ERR_LEAD + 2))
        psum_t = ctx.enter_context(tc.psum_pool(name="psum_t", bufs=2))
        psum_h = ctx.enter_context(tc.psum_pool(name="psum_h", bufs=2))
        psum_acc = ctx.enter_context(tc.psum_pool(name="psum_acc", bufs=1))
        ctx.enter_context(tc.manual_schedule())

        x_rounds = x_pred.rearrange("(c p j) k -> c p (j k)", p=P, j=PACK)
        e_rounds = err.rearrange("(c p j) d -> c p j d", p=P, j=PACK)
        w_raw = const.tile([P, 2, FEATURES], BF16)
        x_raw = []
        e_raw = []

        def load_err(c):
            e_c = raw.tile([P, PACK, FEATURES], BF16, tag="e_raw")
            nc.sync.dma_start(out=e_c[:], in_=e_rounds[c])
            e_raw.append(e_c)

        def load_x(c):
            x_c = raw.tile([P, PACK * FEATURES], BF16, tag="x_raw")
            nc.sync.dma_start(out=x_c[:], in_=x_rounds[c])
            x_raw.append(x_c)

        load_err(0)
        nc.sync.dma_start(out=w_raw[:, 0, :], in_=W_gate)
        nc.sync.dma_start(out=w_raw[:, 1, :], in_=W_up)
        load_x(0)
        for c in range(1, ROUNDS):
            load_err(c)
            load_x(c)

        ident = const.tile([P, P], F32)
        make_identity(nc, ident[:])
        mean_matrix = const.tile([P, P], F32)
        nc.vector.memset(mean_matrix[:], 1.0 / (TOKENS * TOKENS))
        half = const.tile([P, 1], F32)
        nc.vector.memset(half[:], 0.5)
        table_load = const.tile([P, 1], F32)
        nc.scalar.activation(out=table_load[:], in_=half[:], func=ACT.Silu)
        square_sums = const.tile([P, ROUNDS + GRAM_COLS], F32)

        def transpose_words(bank, rows_words):
            for u in range(2):
                nc.tensor.transpose(bank[:, u, :], rows_words[:, u * P : (u + 1) * P], ident[:])

        def interleaved(bank):
            return bank.rearrange("p i u r -> p i r u")

        w_codes = const.tile([P, 2 * HIDDEN], U32, align_bytes=64)
        w_scales = const.tile([P, 2 * HIDDEN], U8, align_bytes=64)

        w_banks = []

        def transpose_weights():
            w_bank = psum_h.tile([P, 2, 2, P], F32, tag="gate", name="w_bank")
            for g in range(2):
                transpose_words(w_bank[:, g], w_raw[:, g, :].bitcast(F32))
            w_banks.append(w_bank)

        w_grouped = const.tile([P, 2 * HIDDEN * PACK], BF16, align_bytes=64)

        def copy_weights():
            nc.scalar.copy(
                out=w_grouped[:].bitcast(F32).rearrange("p (i r u) -> p i r u", i=2, u=2),
                in_=interleaved(w_banks[0][:]),
            )

        def quantise_weights():
            nc.vector.quantize_mx(out=w_codes[:].bitcast(FP8X4), scales=w_scales[:], in_=w_grouped[:])

        x_banks = {}
        x_grouped = {}
        x_quant = {}
        e_grouped = {}
        e_quant = {}
        h_banks = {}
        h_silu = {}
        h_grouped = {}
        h_quant = {}

        def transpose_x(c):
            words = x_raw[c][:].bitcast(F32)
            for b in range(2):
                bank = psum_t.tile([P, 2, 2, P], F32, tag="t")
                for i in range(2):
                    j = 2 * b + i
                    transpose_words(bank[:, i], words[:, j * WORDS : (j + 1) * WORDS])
                x_banks[c, b] = bank

        def copy_x(c):
            grouped = work.tile([P, ROUND * PACK], BF16, tag="x_grouped", align_bytes=64)
            words = grouped[:].bitcast(F32).rearrange("p (b i r u) -> p b i r u", b=2, i=2, u=2)
            nc.scalar.copy(out=words[:, 0], in_=interleaved(x_banks[c, 0][:]))
            if c > 0 and c % VECTOR_COPY_EVERY == 0:
                nc.vector.tensor_copy(out=words[:, 1], in_=interleaved(x_banks[c, 1][:]))
            else:
                nc.scalar.copy(out=words[:, 1], in_=interleaved(x_banks[c, 1][:]))
            x_grouped[c] = grouped

        def parts_of(c):
            return 2 if c == ROUNDS - 1 else 1

        def quantise_x(c, part):
            parts = parts_of(c)
            if part == 0:
                codes = work.tile([P, ROUND], U32, tag="x_codes", align_bytes=64)
                scales = work.tile([P, ROUND], U8, tag="x_scales", align_bytes=64)
                x_quant[c] = (codes, scales)
            codes, scales = x_quant[c]
            width = ROUND // parts
            cols = slice(part * width, (part + 1) * width)
            nc.vector.quantize_mx(
                out=codes[:, cols].bitcast(FP8X4),
                scales=scales[:, cols],
                in_=x_grouped[c][:, part * width * PACK : (part + 1) * width * PACK],
            )

        def first_products(c, part):
            parts = parts_of(c)
            codes, scales = x_quant[c]
            if part == 0:
                gate_bank = psum_h.tile([P, PACK, HIDDEN], F32, tag="gate")
                up_bank = psum_h.tile([P, PACK, HIDDEN], F32, tag="up")
                h_banks[c] = (gate_bank, up_bank)
            for g in (0, 1):
                bank = h_banks[c][g]
                w_cols = slice(g * HIDDEN, (g + 1) * HIDDEN)
                for j in range(part * PACK // parts, (part + 1) * PACK // parts):
                    m_cols = slice(j * P, (j + 1) * P)
                    nc.tensor.matmul_mx(
                        out=bank[:, j, :],
                        lhsT=codes[:, m_cols].bitcast(FP8X4),
                        lhsT_scale=scales[:, m_cols],
                        rhs=w_codes[:, w_cols].bitcast(FP8X4),
                        rhs_scale=w_scales[:, w_cols],
                        start=True,
                        stop=True,
                    )

        def hidden_part(c, part):
            width = HIDDEN // parts_of(c)
            return slice(part * width, (part + 1) * width)

        def silu_gate(c):
            silu = work.tile([P, HIDDEN, PACK], F32, tag="silu")
            for part in range(parts_of(c)):
                w = hidden_part(c, part)
                nc.scalar.activation(
                    out=silu[:, w, :], in_=h_banks[c][0][:, :, w].rearrange("p j w -> p w j"), func=ACT.Silu
                )
            h_silu[c] = silu

        def multiply_up(c):
            grouped = work.tile([P, HIDDEN, PACK], BF16, tag="h_grouped", align_bytes=64)
            for part in range(parts_of(c)):
                w = hidden_part(c, part)
                nc.vector.tensor_tensor(
                    out=grouped[:, w, :],
                    in0=h_silu[c][:, w, :],
                    in1=h_banks[c][1][:, :, w].rearrange("p j w -> p w j"),
                    op=ALU.mult,
                )
            h_grouped[c] = grouped

        def quantise_h(c):
            codes = work.tile([P, HIDDEN], U32, tag="h_codes", align_bytes=64)
            scales = work.tile([P, HIDDEN], U8, tag="h_scales", align_bytes=64)
            for part in range(parts_of(c)):
                w = hidden_part(c, part)
                nc.vector.quantize_mx(
                    out=codes[:, w].bitcast(FP8X4),
                    scales=scales[:, w],
                    in_=h_grouped[c][:, w, :].rearrange("p w j -> p (w j)"),
                )
            h_quant[c] = (codes, scales)

        def group_err(c):
            grouped = work.tile([P, FEATURES, PACK], BF16, tag="e_grouped", align_bytes=64)
            nc.vector.tensor_copy(
                out=grouped[:].rearrange("p (a i) j -> p a j i", i=8),
                in_=e_raw[c][:].rearrange("p j (a i) -> p a j i", i=8),
            )
            e_grouped[c] = grouped

        def quantise_err(c):
            codes = ready.tile([P, FEATURES], U32, tag="e_codes", align_bytes=64)
            scales = ready.tile([P, FEATURES], U8, tag="e_scales", align_bytes=64)
            nc.vector.quantize_mx(
                out=codes[:].bitcast(FP8X4), scales=scales[:], in_=e_grouped[c][:].rearrange("p d j -> p (d j)")
            )
            e_quant[c] = (codes, scales)

        gram = psum_acc.tile([P, GRAM_COLS], F32, tag="gram")

        def gram_blocks(c):
            return 5 if c < FIVE_BLOCK_ROUNDS else 4

        def gram_err(c):
            values = e_raw[c][:].rearrange("p j d -> p (j d)")
            blocks = gram_blocks(c)
            for k in range(blocks):
                block = values[:, k * GRAM_COLS : (k + 1) * GRAM_COLS]
                nc.tensor.matmul(
                    out=gram[:],
                    lhsT=block,
                    rhs=block,
                    start=(c == 0 and k == 0),
                    stop=(c == ROUNDS - 1 and k == blocks - 1),
                )

        def square_err(c):
            first = gram_blocks(c) * GRAM_COLS
            squares = work.tile([P, PACK * FEATURES - 4 * GRAM_COLS], BF16, tag="squares")
            nc.scalar.activation(
                out=squares[:, : PACK * FEATURES - first],
                in_=e_raw[c][:].rearrange("p j d -> p (j d)")[:, first:],
                func=ACT.Square,
                accum_out=square_sums[:, c : c + 1],
            )

        acc = psum_acc.tile([P, FEATURES], F32, tag="acc")
        late_banks = []

        def second_product(c):
            h_codes, h_scales = h_quant[c]
            e_codes, e_scales = e_quant[c]
            if c >= ROUNDS - LATE:
                if not late_banks:
                    late_banks.append(psum_t.tile([P, HIDDEN], F32, tag="t", name="late_0"))
                    late_banks.append(psum_t.tile([P, HIDDEN], F32, tag="t", name="late_1"))
                    late_banks.append(psum_h.tile([P, HIDDEN], F32, tag="gate", name="late_2"))
                    late_banks.append(psum_h.tile([P, HIDDEN], F32, tag="up", name="late_3"))
                for b, bank in enumerate(late_banks):
                    f_cols = slice(b * P, (b + 1) * P)
                    nc.tensor.matmul_mx(
                        out=bank[:],
                        lhsT=e_codes[:, f_cols].bitcast(FP8X4),
                        lhsT_scale=e_scales[:, f_cols],
                        rhs=h_codes[:].bitcast(FP8X4),
                        rhs_scale=h_scales[:],
                        start=(c == ROUNDS - LATE),
                        stop=(c == ROUNDS - 1),
                    )
                return
            nc.tensor.matmul_mx(
                out=acc[:],
                lhsT=h_codes[:].bitcast(FP8X4),
                lhsT_scale=h_scales[:],
                rhs=e_codes[:].bitcast(FP8X4),
                rhs_scale=e_scales[:],
                start=(c == 0),
                stop=(c == ROUNDS - LATE - 1),
            )

        mean_banks = {}
        err_mag = const.tile([P, 1], F32)
        ema = const.tile([P, 1], F32)
        factor = const.tile([P, 1], F32)

        def pick_diagonal():
            nc.vector.tensor_tensor(out=square_sums[:, ROUNDS:], in0=gram[:], in1=ident[:], op=ALU.mult)

        def add_over_partitions():
            mean_bank = psum_acc.tile([P, ROUNDS + GRAM_COLS], F32, tag="gram")
            nc.tensor.matmul(out=mean_bank[:], lhsT=mean_matrix[:], rhs=square_sums[:], start=True, stop=True)
            mean_banks[0] = mean_bank

        def error_magnitude():
            mag_squared = const.tile([P, 1], F32)
            nc.vector.tensor_reduce(out=mag_squared[:], in_=mean_banks[0][:], axis=mybir.AxisListType.X, op=ALU.add)
            nc.gpsimd.tensor_tensor(out=err_mag[:], in0=mag_squared[:], in1=half[:], op=ALU.pow)
            nc.gpsimd.tensor_scalar(
                out=ema[:], in0=err_mag[:], scalar1=0.05 * TOKENS, scalar2=0.95 * TOKENS, op0=ALU.mult, op1=ALU.add
            )

        def gate_factor():
            inverse = const.tile([P, 1], F32)
            nc.vector.reciprocal(out=inverse[:], in_=ema[:])
            nc.gpsimd.tensor_scalar(
                out=factor[:], in0=err_mag[:], scalar1=inverse[:, 0:1], scalar2=3.0 / TOKENS, op0=ALU.mult, op1=ALU.min
            )

        transposed = const.tile([P, FEATURES], F32)
        early_banks = []
        early = const.tile([P, OUT_BLOCKS, HIDDEN], F32)

        def copy_early():
            nc.scalar.copy(out=transposed[:], in_=acc[:])

        def transpose_early():
            bank = psum_acc.tile([P, OUT_BLOCKS, P], F32, tag="acc", name="early_bank")
            for b in range(OUT_BLOCKS):
                nc.tensor.transpose(bank[:, b, :], transposed[:, b * P : (b + 1) * P], ident[:])
            early_banks.append(bank)

        def scale_early():
            for b in (0, 2):
                nc.scalar.activation(
                    out=early[:, b : b + 2, :], in_=early_banks[0][:, b : b + 2, :], func=ACT.Copy, scale=factor[:, 0:1]
                )

        group_err(0)
        gram_err(0)
        square_err(0)
        transpose_weights()
        transpose_x(0)
        copy_weights()
        quantise_err(0)
        copy_x(0)
        transpose_x(1)
        quantise_weights()
        group_err(1)
        quantise_x(0, 0)
        first_products(0, 0)
        quantise_err(1)
        gram_err(1)
        square_err(1)
        for s in range(ROUNDS):
            ahead = s + ERR_LEAD
            if s + 1 < ROUNDS:
                copy_x(s + 1)
            if ahead < ROUNDS:
                group_err(ahead)
            if s + 2 < ROUNDS:
                transpose_x(s + 2)
            silu_gate(s)
            if ahead < ROUNDS:
                gram_err(ahead)
            if s + 1 < ROUNDS:
                for part in range(parts_of(s + 1)):
                    quantise_x(s + 1, part)
                    first_products(s + 1, part)
            if ahead == ROUNDS - 1:
                pick_diagonal()
            if s == ROUNDS - 2:
                error_magnitude()
            multiply_up(s)
            if ahead < ROUNDS:
                quantise_err(ahead)
                square_err(ahead)
            if s == ROUNDS - 2:
                gate_factor()
            if ahead == ROUNDS - 1:
                add_over_partitions()
            if s == ROUNDS - LATE:
                copy_early()
                transpose_early()
            quantise_h(s)
            second_product(s)
        scale_early()

        result = const.tile([P, OUT_BLOCKS, HIDDEN], F32)
        out_blocks = out.rearrange("(b p) w -> p b w", p=P)
        for b in range(OUT_BLOCKS):
            nc.vector.scalar_tensor_tensor(
                out=result[:, b, :],
                in0=late_banks[b][:],
                scalar=factor[:, 0:1],
                in1=early[:, b, :],
                op0=ALU.mult,
                op1=ALU.add,
            )
            if b % 2 == 1:
                nc.sync.dma_start(out=out_blocks[:, b - 1 : b + 1, :], in_=result[:, b - 1 : b + 1, :])
